import numpy as np
import ml_dtypes


def mxq(x, axis, fmt="e4m3"):
    dtype, down = {"e4m3": (ml_dtypes.float8_e4m3fn, 7), "e5m2": (ml_dtypes.float8_e5m2, 14)}[fmt]
    v = np.moveaxis(np.asarray(x, np.float32).astype(ml_dtypes.bfloat16).astype(np.float64), axis, -1)
    blocks = v.reshape(v.shape[:-1] + (-1, 32))
    amax = np.abs(blocks).max(-1, keepdims=True)
    byte = np.maximum(np.where(amax > 0, np.frexp(amax)[1] - 1 + 127, 0) - down, 1)
    scale = np.exp2(byte - 127.0)
    codes = (blocks / scale).astype(np.float32).astype(dtype).astype(np.float64)
    return np.moveaxis((codes * scale).reshape(v.shape), -1, axis)


WIDE = False


def mx_kscale(k):
    if not WIDE:
        return np.ones(k)
    levels = np.array([20, -20, 10, -10, 0])
    a = np.random.permutation(np.resize(levels, k // 512 * 4)).reshape(k // 512, 4)
    idx = np.arange(k)
    return np.exp2(a[idx // 512, idx % 128 // 32])


BF16 = ml_dtypes.bfloat16


def bf(x):
    return np.asarray(x, np.float32).astype(BF16)


def f64(x):
    return np.asarray(x).astype(np.float64)


N, P, D, E, F = 512, 3, 128, 512, 1024


def setup_inputs():
    u = mx_kscale(E)
    x = np.random.standard_normal((N, P, D)) + 0.5 * np.random.standard_normal((1, P, D))
    w1a = np.random.standard_normal((D, E)) / np.sqrt(D) / u[None, :]
    w2a = np.random.standard_normal((D, E)) / np.sqrt(D) / u[None, :]
    g = np.random.standard_normal((N, P, E)) * np.exp2(np.random.randint(-12, 1, (N, P, 1))) * 4.0 * u
    return {"x": bf(x), "w1a": bf(w1a), "w2a": bf(w2a), "grad_out": bf(g)}


def reference(x, w1a, w2a, grad_out):
    gq = mxq(f64(grad_out), 2, "e5m2")
    a = gq @ mxq(f64(w2a), 1, "e4m3").T
    b = gq @ mxq(f64(w1a), 1, "e4m3").T
    return a + (b.sum(axis=1, keepdims=True) - b) * 0.5

@@ -1,0 +1,134 @@
+import concourse.mybir as mybir
+from concourse.masks import make_identity
+
+F32 = mybir.dt.float32
+BF16 = mybir.dt.bfloat16
+I32 = mybir.dt.int32
+U32 = mybir.dt.uint32
+U8 = mybir.dt.uint8
+E5M2_X4 = mybir.dt.float8_e5m2_x4
+E4M3_X4 = mybir.dt.float8_e4m3fn_x4
+
+P = 128
+ITEMS = 512
+HOPS = 3
+E = 512
+ITEM_BLOCKS = ITEMS // P
+HALVES = 2
+WORDS = E // 2
+N_MOVING = 512
+W_BLOCKS = 6
+W2_BLOCK = 2
+
+FLOPS = 2 * 2 * ITEMS * HOPS * E * P
+BYTES = 2 * (2 * P * E + ITEMS * HOPS * E) + 4 * ITEMS * HOPS * P
+
+
+def tile_dogtaitujuanji_pa_s_kernel(tc, x, w1a, w2a, grad_out, out):
+    nc = tc.nc
+    with (
+        tc.tile_pool(name="resident", bufs=1) as resident,
+        tc.tile_pool(name="stream", bufs=4) as stream,
+        tc.psum_pool(name="flipped_banks", bufs=4) as flipped_banks,
+        tc.psum_pool(name="sum_banks", bufs=4) as sum_banks,
+    ):
+        w1_rows = resident.tile([P, E], BF16)
+        nc.sync.dma_start(out=w1_rows[:], in_=w1a)
+        w2_rows = resident.tile([P, E], BF16)
+        nc.sync.dma_start(out=w2_rows[:], in_=w2a)
+        g_rows = resident.tile([P, ITEM_BLOCKS * HOPS * E], BF16)
+        for unit in range(ITEM_BLOCKS * HOPS):
+            block, hop = divmod(unit, HOPS)
+            nc.sync.dma_start(
+                out=g_rows[:, unit * E : (unit + 1) * E],
+                in_=grad_out[block * P : (block + 1) * P, hop, :],
+            )
+        g_words = g_rows[:].bitcast(F32)
+
+        identity = resident.tile([P, P], F32)
+        make_identity(nc, identity[:])
+
+        w_codes = resident.tile([P, W_BLOCKS * P], U32, align_bytes=64)
+        w_scales = resident.tile([P, W_BLOCKS * P], U8, align_bytes=64)
+        g_codes = resident.tile([P, ITEM_BLOCKS * HOPS * P], U32, align_bytes=64)
+        g_scales = resident.tile([P, ITEM_BLOCKS * HOPS * P], U8, align_bytes=64)
+
+        def flip(words):
+            flipped = flipped_banks.tile([P, HALVES * P], F32)
+            for half in range(HALVES):
+                nc.tensor.transpose(
+                    out=flipped[:, half * P : (half + 1) * P],
+                    in_=words[:, half * P : (half + 1) * P],
+                    identity=identity[:],
+                )
+            return flipped
+
+        last = (W_BLOCKS - 1) * P
+        nc.vector.memset(w_codes[:, last:].bitcast(I32), 0)
+        nc.vector.memset(w_scales[:, last:].bitcast(I32), 0)
+
+        w1_flipped = flip(w1_rows[:].bitcast(F32))
+        w1_grouped = resident.tile([P, P * 4], BF16, align_bytes=64)
+        nc.vector.tensor_scalar_mul(
+            out=w1_grouped[:].rearrange("p (d h e) -> p d h e", h=HALVES, e=2),
+            in0=w1_flipped[:].bitcast(BF16).rearrange("p (h d e) -> p d h e", h=HALVES, e=2),
+            scalar1=0.5,
+        )
+        w2_flipped = flip(w2_rows[:].bitcast(F32))
+        w2_grouped = resident.tile([P, P * 4], BF16, align_bytes=64)
+        nc.scalar.copy(
+            out=w2_grouped[:].bitcast(F32).rearrange("p (d h) -> p d h", h=HALVES),
+            in_=w2_flipped[:].rearrange("p (h d) -> p d h", h=HALVES),
+        )
+        for w_block in reversed(range(W_BLOCKS - 1)):
+            grouped = w2_grouped if w_block == W2_BLOCK else w1_grouped
+            cols = slice(w_block * P, (w_block + 1) * P)
+            nc.vector.quantize_mx(
+                out=w_codes[:, cols].bitcast(E4M3_X4),
+                scales=w_scales[:, cols],
+                in_=grouped[:],
+            )
+
+        def prepare(block):
+            for unit in range(block * HOPS, (block + 1) * HOPS):
+                g_flipped = flip(g_words[:, unit * WORDS : (unit + 1) * WORDS])
+                g_grouped = stream.tile([P, P * 4], BF16, align_bytes=64)
+                nc.scalar.copy(
+                    out=g_grouped[:].bitcast(F32).rearrange("p (n h) -> p n h", h=HALVES),
+                    in_=g_flipped[:].rearrange("p (h n) -> p n h", h=HALVES),
+                )
+                cols = slice(unit * P, (unit + 1) * P)
+                nc.vector.quantize_mx(
+                    out=g_codes[:, cols].bitcast(E5M2_X4),
+                    scales=g_scales[:, cols],
+                    in_=g_grouped[:],
+                )
+
+        def multiply(block):
+            sums = sum_banks.tile([P, N_MOVING], F32)
+            for hop in range(HOPS):
+                unit = block * HOPS + hop
+                cols = slice(unit * P, (unit + 1) * P)
+                first = (W2_BLOCK - hop) * P
+                window = slice(first, first + N_MOVING)
+                nc.tensor.matmul_mx(
+                    out=sums[:],
+                    lhsT=g_codes[:, cols].bitcast(E5M2_X4),
+                    lhsT_scale=g_scales[:, cols],
+                    rhs=w_codes[:, window].bitcast(E4M3_X4),
+                    rhs_scale=w_scales[:, window],
+                    start=(hop == 0),
+                    stop=(hop == HOPS - 1),
+                )
+            result = stream.tile([P, HOPS * P], F32)
+            nc.vector.tensor_copy(out=result[:], in_=sums[:, : HOPS * P])
+            nc.sync.dma_start(
+                out=out[block * P : (block + 1) * P, :, :].rearrange("n p d -> n (p d)"),
+                in_=result[:],
+            )
+
+        prepare(0)
+        for block in range(ITEM_BLOCKS):
+            if block + 1 < ITEM_BLOCKS:
+                prepare(block + 1)
+            multiply(block)

@@ -19,6 +19,7 @@ WORDS = E // 2
 N_MOVING = 512
 W_BLOCKS = 6
 W2_BLOCK = 2
+RUN_BLOCKS = 2
 
 FLOPS = 2 * 2 * ITEMS * HOPS * E * P
 BYTES = 2 * (2 * P * E + ITEMS * HOPS * E) + 4 * ITEMS * HOPS * P
@@ -31,17 +32,17 @@ def tile_dogtaitujuanji_pa_s_kernel(tc, x, w1a, w2a, grad_out, out):
         tc.tile_pool(name="stream", bufs=4) as stream,
         tc.psum_pool(name="flipped_banks", bufs=4) as flipped_banks,
         tc.psum_pool(name="sum_banks", bufs=4) as sum_banks,
+        tc.manual_schedule(),
     ):
         w1_rows = resident.tile([P, E], BF16)
         nc.sync.dma_start(out=w1_rows[:], in_=w1a)
         w2_rows = resident.tile([P, E], BF16)
         nc.sync.dma_start(out=w2_rows[:], in_=w2a)
         g_rows = resident.tile([P, ITEM_BLOCKS * HOPS * E], BF16)
-        for unit in range(ITEM_BLOCKS * HOPS):
-            block, hop = divmod(unit, HOPS)
+        for block in range(ITEM_BLOCKS):
             nc.sync.dma_start(
-                out=g_rows[:, unit * E : (unit + 1) * E],
-                in_=grad_out[block * P : (block + 1) * P, hop, :],
+                out=g_rows[:, block * HOPS * E : (block + 1) * HOPS * E],
+                in_=grad_out[block * P : (block + 1) * P, :, :].rearrange("n p e -> n (p e)"),
             )
         g_words = g_rows[:].bitcast(F32)
 
@@ -127,8 +128,8 @@ def tile_dogtaitujuanji_pa_s_kernel(tc, x, w1a, w2a, grad_out, out):
                 in_=result[:],
             )
 
-        prepare(0)
-        for block in range(ITEM_BLOCKS):
-            if block + 1 < ITEM_BLOCKS:
-                prepare(block + 1)
-            multiply(block)
+        for first_block in range(0, ITEM_BLOCKS, RUN_BLOCKS):
+            for block in range(first_block, first_block + RUN_BLOCKS):
+                prepare(block)
+            for block in range(first_block, first_block + RUN_BLOCKS):
+                multiply(block)

@@ -13,13 +13,16 @@ P = 128
 ITEMS = 512
 HOPS = 3
 E = 512
+PACK = 4
 ITEM_BLOCKS = ITEMS // P
+UNITS = ITEM_BLOCKS * HOPS
 HALVES = 2
 WORDS = E // 2
-N_MOVING = 512
+N_MOVING = 4 * P
 W_BLOCKS = 6
 W2_BLOCK = 2
-RUN_BLOCKS = 2
+LEAD_BLOCKS = 2
+WARM_UP = 4
 
 FLOPS = 2 * 2 * ITEMS * HOPS * E * P
 BYTES = 2 * (2 * P * E + ITEMS * HOPS * E) + 4 * ITEMS * HOPS * P
@@ -31,28 +34,37 @@ def tile_dogtaitujuanji_pa_s_kernel(tc, x, w1a, w2a, grad_out, out):
         tc.tile_pool(name="resident", bufs=1) as resident,
         tc.tile_pool(name="stream", bufs=4) as stream,
         tc.psum_pool(name="flipped_banks", bufs=4) as flipped_banks,
-        tc.psum_pool(name="sum_banks", bufs=4) as sum_banks,
+        tc.psum_pool(name="sum_banks", bufs=3) as sum_banks,
+        tc.psum_pool(name="idle_bank", bufs=1) as idle_bank,
         tc.manual_schedule(),
     ):
         w1_rows = resident.tile([P, E], BF16)
         nc.sync.dma_start(out=w1_rows[:], in_=w1a)
         w2_rows = resident.tile([P, E], BF16)
         nc.sync.dma_start(out=w2_rows[:], in_=w2a)
-        g_rows = resident.tile([P, ITEM_BLOCKS * HOPS * E], BF16)
-        for block in range(ITEM_BLOCKS):
+        g_rows = resident.tile([P, UNITS * E], BF16)
+        for unit in range(UNITS):
+            block, hop = divmod(unit, HOPS)
             nc.sync.dma_start(
-                out=g_rows[:, block * HOPS * E : (block + 1) * HOPS * E],
-                in_=grad_out[block * P : (block + 1) * P, :, :].rearrange("n p e -> n (p e)"),
+                out=g_rows[:, unit * E : (unit + 1) * E],
+                in_=grad_out[block * P : (block + 1) * P, hop, :],
             )
         g_words = g_rows[:].bitcast(F32)
 
+        zeros = resident.tile([P, P], F32)
+        nc.vector.memset(zeros[:], 0.0)
+        unread = idle_bank.tile([P, P], F32)
+
+        def idle_matmuls(count):
+            for repeat in range(count):
+                nc.tensor.matmul(
+                    out=unread[:], lhsT=zeros[:], rhs=zeros[:], start=True, stop=True
+                )
+
+        idle_matmuls(WARM_UP)
+
         identity = resident.tile([P, P], F32)
         make_identity(nc, identity[:])
-
-        w_codes = resident.tile([P, W_BLOCKS * P], U32, align_bytes=64)
-        w_scales = resident.tile([P, W_BLOCKS * P], U8, align_bytes=64)
-        g_codes = resident.tile([P, ITEM_BLOCKS * HOPS * P], U32, align_bytes=64)
-        g_scales = resident.tile([P, ITEM_BLOCKS * HOPS * P], U8, align_bytes=64)
 
         def flip(words):
             flipped = flipped_banks.tile([P, HALVES * P], F32)
@@ -64,22 +76,24 @@ def tile_dogtaitujuanji_pa_s_kernel(tc, x, w1a, w2a, grad_out, out):
                 )
             return flipped
 
-        last = (W_BLOCKS - 1) * P
-        nc.vector.memset(w_codes[:, last:].bitcast(I32), 0)
-        nc.vector.memset(w_scales[:, last:].bitcast(I32), 0)
+        w_codes = resident.tile([P, W_BLOCKS * P], U32, align_bytes=64)
+        w_scales = resident.tile([P, W_BLOCKS * P], U8, align_bytes=64)
+        zero_block = slice((W_BLOCKS - 1) * P, W_BLOCKS * P)
+        nc.vector.memset(w_codes[:, zero_block].bitcast(I32), 0)
+        nc.vector.memset(w_scales[:, zero_block].bitcast(I32), 0)
 
         w1_flipped = flip(w1_rows[:].bitcast(F32))
-        w1_grouped = resident.tile([P, P * 4], BF16, align_bytes=64)
+        w1_grouped = resident.tile([P, P * PACK], BF16, align_bytes=64)
         nc.vector.tensor_scalar_mul(
-            out=w1_grouped[:].rearrange("p (d h e) -> p d h e", h=HALVES, e=2),
-            in0=w1_flipped[:].bitcast(BF16).rearrange("p (h d e) -> p d h e", h=HALVES, e=2),
+            out=w1_grouped[:].rearrange("w (d h e) -> w d h e", h=HALVES, e=2),
+            in0=w1_flipped[:].bitcast(BF16).rearrange("w (h d e) -> w d h e", h=HALVES, e=2),
             scalar1=0.5,
         )
         w2_flipped = flip(w2_rows[:].bitcast(F32))
-        w2_grouped = resident.tile([P, P * 4], BF16, align_bytes=64)
+        w2_grouped = resident.tile([P, P * PACK], BF16, align_bytes=64)
         nc.scalar.copy(
-            out=w2_grouped[:].bitcast(F32).rearrange("p (d h) -> p d h", h=HALVES),
-            in_=w2_flipped[:].rearrange("p (h d) -> p d h", h=HALVES),
+            out=w2_grouped[:].bitcast(F32).rearrange("w (d h) -> w d h", h=HALVES),
+            in_=w2_flipped[:].rearrange("w (h d) -> w d h", h=HALVES),
         )
         for w_block in reversed(range(W_BLOCKS - 1)):
             grouped = w2_grouped if w_block == W2_BLOCK else w1_grouped
@@ -90,20 +104,22 @@ def tile_dogtaitujuanji_pa_s_kernel(tc, x, w1a, w2a, grad_out, out):
                 in_=grouped[:],
             )
 
-        def prepare(block):
-            for unit in range(block * HOPS, (block + 1) * HOPS):
-                g_flipped = flip(g_words[:, unit * WORDS : (unit + 1) * WORDS])
-                g_grouped = stream.tile([P, P * 4], BF16, align_bytes=64)
-                nc.scalar.copy(
-                    out=g_grouped[:].bitcast(F32).rearrange("p (n h) -> p n h", h=HALVES),
-                    in_=g_flipped[:].rearrange("p (h n) -> p n h", h=HALVES),
-                )
-                cols = slice(unit * P, (unit + 1) * P)
-                nc.vector.quantize_mx(
-                    out=g_codes[:, cols].bitcast(E5M2_X4),
-                    scales=g_scales[:, cols],
-                    in_=g_grouped[:],
-                )
+        g_codes = resident.tile([P, UNITS * P], U32, align_bytes=64)
+        g_scales = resident.tile([P, UNITS * P], U8, align_bytes=64)
+
+        def prepare(unit):
+            g_flipped = flip(g_words[:, unit * WORDS : (unit + 1) * WORDS])
+            g_grouped = stream.tile([P, P * PACK], BF16, align_bytes=64)
+            nc.scalar.copy(
+                out=g_grouped[:].bitcast(F32).rearrange("w (n h) -> w n h", h=HALVES),
+                in_=g_flipped[:].rearrange("w (h n) -> w n h", h=HALVES),
+            )
+            cols = slice(unit * P, (unit + 1) * P)
+            nc.vector.quantize_mx(
+                out=g_codes[:, cols].bitcast(E5M2_X4),
+                scales=g_scales[:, cols],
+                in_=g_grouped[:],
+            )
 
         def multiply(block):
             sums = sum_banks.tile([P, N_MOVING], F32)
@@ -128,8 +144,13 @@ def tile_dogtaitujuanji_pa_s_kernel(tc, x, w1a, w2a, grad_out, out):
                 in_=result[:],
             )
 
-        for first_block in range(0, ITEM_BLOCKS, RUN_BLOCKS):
-            for block in range(first_block, first_block + RUN_BLOCKS):
-                prepare(block)
-            for block in range(first_block, first_block + RUN_BLOCKS):
-                multiply(block)
+        for unit in range(LEAD_BLOCKS * HOPS):
+            if unit % 2 == 0:
+                idle_matmuls(1)
+            prepare(unit)
+        for block in range(ITEM_BLOCKS):
+            multiply(block)
+            ahead = block + LEAD_BLOCKS
+            if ahead < ITEM_BLOCKS:
+                for unit in range(ahead * HOPS, (ahead + 1) * HOPS):
+                    prepare(unit)

@@ -43,11 +43,16 @@ def tile_dogtaitujuanji_pa_s_kernel(tc, x, w1a, w2a, grad_out, out):
         w2_rows = resident.tile([P, E], BF16)
         nc.sync.dma_start(out=w2_rows[:], in_=w2a)
         g_rows = resident.tile([P, UNITS * E], BF16)
-        for unit in range(UNITS):
+        for unit in range(LEAD_BLOCKS * HOPS):
             block, hop = divmod(unit, HOPS)
             nc.sync.dma_start(
                 out=g_rows[:, unit * E : (unit + 1) * E],
                 in_=grad_out[block * P : (block + 1) * P, hop, :],
+            )
+        for block in range(LEAD_BLOCKS, ITEM_BLOCKS):
+            nc.sync.dma_start(
+                out=g_rows[:, block * HOPS * E : (block + 1) * HOPS * E],
+                in_=grad_out[block * P : (block + 1) * P, :, :].rearrange("n p e -> n (p e)"),
             )
         g_words = g_rows[:].bitcast(F32)
 

@@ -38,26 +38,32 @@ def tile_dogtaitujuanji_pa_s_kernel(tc, x, w1a, w2a, grad_out, out):
         tc.psum_pool(name="idle_bank", bufs=1) as idle_bank,
         tc.manual_schedule(),
     ):
-        w1_rows = resident.tile([P, E], BF16)
-        nc.sync.dma_start(out=w1_rows[:], in_=w1a)
-        w2_rows = resident.tile([P, E], BF16)
-        nc.sync.dma_start(out=w2_rows[:], in_=w2a)
-        g_rows = resident.tile([P, UNITS * E], BF16)
-        for unit in range(LEAD_BLOCKS * HOPS):
-            block, hop = divmod(unit, HOPS)
-            nc.sync.dma_start(
-                out=g_rows[:, unit * E : (unit + 1) * E],
-                in_=grad_out[block * P : (block + 1) * P, hop, :],
-            )
-        for block in range(LEAD_BLOCKS, ITEM_BLOCKS):
-            nc.sync.dma_start(
-                out=g_rows[:, block * HOPS * E : (block + 1) * HOPS * E],
-                in_=grad_out[block * P : (block + 1) * P, :, :].rearrange("n p e -> n (p e)"),
-            )
-        g_words = g_rows[:].bitcast(F32)
-
         zeros = resident.tile([P, P], F32)
         nc.vector.memset(zeros[:], 0.0)
+        w1_rows = resident.tile([P, E], BF16)
+        w2_rows = resident.tile([P, E], BF16)
+        g_rows = resident.tile([P, UNITS * E], BF16)
+
+        def load_units(queue, first, last):
+            block = first // HOPS
+            nc_queue = queue
+            nc_queue.dma_start(
+                out=g_rows[:, first * E : last * E],
+                in_=grad_out[
+                    block * P : (block + 1) * P, first - block * HOPS : last - block * HOPS, :
+                ].rearrange("n p e -> n (p e)"),
+            )
+        nc.sync.dma_start(out=w1_rows[:], in_=w1a)
+        nc.sync.dma_start(out=w2_rows[:], in_=w2a)
+        load_units(nc.sync, 0, 1)
+        load_units(nc.sync, 1, 2)
+        load_units(nc.sync, 2, 3)
+        load_units(nc.sync, 3, 4)
+        load_units(nc.sync, 4, 5)
+        load_units(nc.sync, 5, 6)
+        load_units(nc.sync, 6, 9)
+        load_units(nc.sync, 9, 12)
+        g_words = g_rows[:].bitcast(F32)
         unread = idle_bank.tile([P, P], F32)
 
         def idle_matmuls(count):
@@ -66,7 +72,7 @@ def tile_dogtaitujuanji_pa_s_kernel(tc, x, w1a, w2a, grad_out, out):
                     out=unread[:], lhsT=zeros[:], rhs=zeros[:], start=True, stop=True
                 )
 
-        idle_matmuls(WARM_UP)
+        idle_matmuls(3)
 
         identity = resident.tile([P, P], F32)
         make_identity(nc, identity[:])
@@ -86,21 +92,25 @@ def tile_dogtaitujuanji_pa_s_kernel(tc, x, w1a, w2a, grad_out, out):
         zero_block = slice((W_BLOCKS - 1) * P, W_BLOCKS * P)
         nc.vector.memset(w_codes[:, zero_block].bitcast(I32), 0)
         nc.vector.memset(w_scales[:, zero_block].bitcast(I32), 0)
-
-        w1_flipped = flip(w1_rows[:].bitcast(F32))
         w1_grouped = resident.tile([P, P * PACK], BF16, align_bytes=64)
-        nc.vector.tensor_scalar_mul(
-            out=w1_grouped[:].rearrange("w (d h e) -> w d h e", h=HALVES, e=2),
-            in0=w1_flipped[:].bitcast(BF16).rearrange("w (h d e) -> w d h e", h=HALVES, e=2),
-            scalar1=0.5,
-        )
-        w2_flipped = flip(w2_rows[:].bitcast(F32))
         w2_grouped = resident.tile([P, P * PACK], BF16, align_bytes=64)
-        nc.scalar.copy(
-            out=w2_grouped[:].bitcast(F32).rearrange("w (d h) -> w d h", h=HALVES),
-            in_=w2_flipped[:].rearrange("w (h d) -> w d h", h=HALVES),
-        )
-        for w_block in reversed(range(W_BLOCKS - 1)):
+
+        def flip_w1():
+            w1_flipped = flip(w1_rows[:].bitcast(F32))
+            nc.vector.tensor_scalar_mul(
+                out=w1_grouped[:].rearrange("w (d h e) -> w d h e", h=HALVES, e=2),
+                in0=w1_flipped[:].bitcast(BF16).rearrange("w (h d e) -> w d h e", h=HALVES, e=2),
+                scalar1=0.5,
+            )
+
+        def flip_w2():
+            w2_flipped = flip(w2_rows[:].bitcast(F32))
+            nc.scalar.copy(
+                out=w2_grouped[:].bitcast(F32).rearrange("w (d h) -> w d h", h=HALVES),
+                in_=w2_flipped[:].rearrange("w (h d) -> w d h", h=HALVES),
+            )
+
+        def quantise_w(w_block):
             grouped = w2_grouped if w_block == W2_BLOCK else w1_grouped
             cols = slice(w_block * P, (w_block + 1) * P)
             nc.vector.quantize_mx(
@@ -111,22 +121,27 @@ def tile_dogtaitujuanji_pa_s_kernel(tc, x, w1a, w2a, grad_out, out):
 
         g_codes = resident.tile([P, UNITS * P], U32, align_bytes=64)
         g_scales = resident.tile([P, UNITS * P], U8, align_bytes=64)
+        grouped_of = {}
 
-        def prepare(unit):
+        def flip_unit(unit, on_vector):
             g_flipped = flip(g_words[:, unit * WORDS : (unit + 1) * WORDS])
             g_grouped = stream.tile([P, P * PACK], BF16, align_bytes=64)
-            nc.scalar.copy(
+            copy = nc.vector.tensor_copy if on_vector else nc.scalar.copy
+            copy(
                 out=g_grouped[:].bitcast(F32).rearrange("w (n h) -> w n h", h=HALVES),
                 in_=g_flipped[:].rearrange("w (h n) -> w n h", h=HALVES),
             )
+            grouped_of[unit] = g_grouped
+
+        def quantise_unit(unit):
             cols = slice(unit * P, (unit + 1) * P)
             nc.vector.quantize_mx(
                 out=g_codes[:, cols].bitcast(E5M2_X4),
                 scales=g_scales[:, cols],
-                in_=g_grouped[:],
+                in_=grouped_of[unit][:],
             )
 
-        def multiply(block):
+        def passes(block):
             sums = sum_banks.tile([P, N_MOVING], F32)
             for hop in range(HOPS):
                 unit = block * HOPS + hop
@@ -142,20 +157,53 @@ def tile_dogtaitujuanji_pa_s_kernel(tc, x, w1a, w2a, grad_out, out):
                     start=(hop == 0),
                     stop=(hop == HOPS - 1),
                 )
-            result = stream.tile([P, HOPS * P], F32)
-            nc.vector.tensor_copy(out=result[:], in_=sums[:, : HOPS * P])
-            nc.sync.dma_start(
-                out=out[block * P : (block + 1) * P, :, :].rearrange("n p d -> n (p d)"),
-                in_=result[:],
-            )
+            return sums
 
-        for unit in range(LEAD_BLOCKS * HOPS):
-            if unit % 2 == 0:
-                idle_matmuls(1)
-            prepare(unit)
-        for block in range(ITEM_BLOCKS):
-            multiply(block)
-            ahead = block + LEAD_BLOCKS
-            if ahead < ITEM_BLOCKS:
-                for unit in range(ahead * HOPS, (ahead + 1) * HOPS):
-                    prepare(unit)
+        def leave(block, sums, pieces, engines, queues):
+            result = stream.tile([P, HOPS * P], F32)
+            out_rows = out[block * P : (block + 1) * P, :, :].rearrange("n p d -> n (p d)")
+            width = HOPS * P // pieces
+            for piece in range(pieces):
+                cols = slice(piece * width, (piece + 1) * width)
+                engines[piece % len(engines)](out=result[:, cols], in_=sums[:, cols])
+                queues[piece % len(queues)].dma_start(out=out_rows[:, cols], in_=result[:, cols])
+
+        flip_w1()
+        idle_matmuls(1)
+        flip_w2()
+        quantise_w(4)
+        quantise_w(3)
+        quantise_w(2)
+        quantise_w(1)
+        quantise_w(0)
+        idle_matmuls(1)
+        flip_unit(0, False)
+        quantise_unit(0)
+        flip_unit(1, False)
+        quantise_unit(1)
+        idle_matmuls(1)
+        flip_unit(2, False)
+        quantise_unit(2)
+        flip_unit(3, False)
+        quantise_unit(3)
+        idle_matmuls(1)
+        flip_unit(4, False)
+        quantise_unit(4)
+        flip_unit(5, False)
+        quantise_unit(5)
+        leave(0, passes(0), 1, (nc.vector.tensor_copy,), (nc.sync,))
+        flip_unit(6, False)
+        quantise_unit(6)
+        flip_unit(7, False)
+        quantise_unit(7)
+        flip_unit(8, False)
+        quantise_unit(8)
+        leave(1, passes(1), 1, (nc.vector.tensor_copy,), (nc.sync,))
+        flip_unit(9, False)
+        quantise_unit(9)
+        flip_unit(10, False)
+        quantise_unit(10)
+        flip_unit(11, False)
+        quantise_unit(11)
+        leave(2, passes(2), 1, (nc.vector.tensor_copy,), (nc.sync,))
+        leave(3, passes(3), 1, (nc.vector.tensor_copy,), (nc.sync,))

@@ -72,7 +72,7 @@ def tile_dogtaitujuanji_pa_s_kernel(tc, x, w1a, w2a, grad_out, out):
                     out=unread[:], lhsT=zeros[:], rhs=zeros[:], start=True, stop=True
                 )
 
-        idle_matmuls(3)
+        idle_matmuls(2)
 
         identity = resident.tile([P, P], F32)
         make_identity(nc, identity[:])

import concourse.mybir as mybir
from concourse.masks import make_identity

F32 = mybir.dt.float32
BF16 = mybir.dt.bfloat16
I32 = mybir.dt.int32
U32 = mybir.dt.uint32
U8 = mybir.dt.uint8
E5M2_X4 = mybir.dt.float8_e5m2_x4
E4M3_X4 = mybir.dt.float8_e4m3fn_x4

P = 128
ITEMS = 512
HOPS = 3
E = 512
PACK = 4
ITEM_BLOCKS = ITEMS // P
UNITS = ITEM_BLOCKS * HOPS
HALVES = 2
WORDS = E // 2
N_MOVING = 4 * P
W_BLOCKS = 6
W2_BLOCK = 2
LEAD_BLOCKS = 2
WARM_UP = 4

FLOPS = 2 * 2 * ITEMS * HOPS * E * P
BYTES = 2 * (2 * P * E + ITEMS * HOPS * E) + 4 * ITEMS * HOPS * P


def tile_dogtaitujuanji_pa_s_kernel(tc, x, w1a, w2a, grad_out, out):
    nc = tc.nc
    with (
        tc.tile_pool(name="resident", bufs=1) as resident,
        tc.tile_pool(name="stream", bufs=4) as stream,
        tc.psum_pool(name="flipped_banks", bufs=4) as flipped_banks,
        tc.psum_pool(name="sum_banks", bufs=3) as sum_banks,
        tc.psum_pool(name="idle_bank", bufs=1) as idle_bank,
        tc.manual_schedule(),
    ):
        zeros = resident.tile([P, P], F32)
        nc.vector.memset(zeros[:], 0.0)
        w1_rows = resident.tile([P, E], BF16)
        w2_rows = resident.tile([P, E], BF16)
        g_rows = resident.tile([P, UNITS * E], BF16)

        def load_units(queue, first, last):
            block = first // HOPS
            nc_queue = queue
            nc_queue.dma_start(
                out=g_rows[:, first * E : last * E],
                in_=grad_out[
                    block * P : (block + 1) * P, first - block * HOPS : last - block * HOPS, :
                ].rearrange("n p e -> n (p e)"),
            )
        nc.sync.dma_start(out=w1_rows[:], in_=w1a)
        nc.sync.dma_start(out=w2_rows[:], in_=w2a)
        load_units(nc.sync, 0, 1)
        load_units(nc.sync, 1, 2)
        load_units(nc.sync, 2, 3)
        load_units(nc.sync, 3, 4)
        load_units(nc.sync, 4, 5)
        load_units(nc.sync, 5, 6)
        load_units(nc.sync, 6, 9)
        load_units(nc.sync, 9, 12)
        g_words = g_rows[:].bitcast(F32)
        unread = idle_bank.tile([P, P], F32)

        def idle_matmuls(count):
            for repeat in range(count):
                nc.tensor.matmul(
                    out=unread[:], lhsT=zeros[:], rhs=zeros[:], start=True, stop=True
                )

        idle_matmuls(2)

        identity = resident.tile([P, P], F32)
        make_identity(nc, identity[:])

        def flip(words):
            flipped = flipped_banks.tile([P, HALVES * P], F32)
            for half in range(HALVES):
                nc.tensor.transpose(
                    out=flipped[:, half * P : (half + 1) * P],
                    in_=words[:, half * P : (half + 1) * P],
                    identity=identity[:],
                )
            return flipped

        w_codes = resident.tile([P, W_BLOCKS * P], U32, align_bytes=64)
        w_scales = resident.tile([P, W_BLOCKS * P], U8, align_bytes=64)
        zero_block = slice((W_BLOCKS - 1) * P, W_BLOCKS * P)
        nc.vector.memset(w_codes[:, zero_block].bitcast(I32), 0)
        nc.vector.memset(w_scales[:, zero_block].bitcast(I32), 0)
        w1_grouped = resident.tile([P, P * PACK], BF16, align_bytes=64)
        w2_grouped = resident.tile([P, P * PACK], BF16, align_bytes=64)

        def flip_w1():
            w1_flipped = flip(w1_rows[:].bitcast(F32))
            nc.vector.tensor_scalar_mul(
                out=w1_grouped[:].rearrange("w (d h e) -> w d h e", h=HALVES, e=2),
                in0=w1_flipped[:].bitcast(BF16).rearrange("w (h d e) -> w d h e", h=HALVES, e=2),
                scalar1=0.5,
            )

        def flip_w2():
            w2_flipped = flip(w2_rows[:].bitcast(F32))
            nc.scalar.copy(
                out=w2_grouped[:].bitcast(F32).rearrange("w (d h) -> w d h", h=HALVES),
                in_=w2_flipped[:].rearrange("w (h d) -> w d h", h=HALVES),
            )

        def quantise_w(w_block):
            grouped = w2_grouped if w_block == W2_BLOCK else w1_grouped
            cols = slice(w_block * P, (w_block + 1) * P)
            nc.vector.quantize_mx(
                out=w_codes[:, cols].bitcast(E4M3_X4),
                scales=w_scales[:, cols],
                in_=grouped[:],
            )

        g_codes = resident.tile([P, UNITS * P], U32, align_bytes=64)
        g_scales = resident.tile([P, UNITS * P], U8, align_bytes=64)
        grouped_of = {}

        def flip_unit(unit, on_vector):
            g_flipped = flip(g_words[:, unit * WORDS : (unit + 1) * WORDS])
            g_grouped = stream.tile([P, P * PACK], BF16, align_bytes=64)
            copy = nc.vector.tensor_copy if on_vector else nc.scalar.copy
            copy(
                out=g_grouped[:].bitcast(F32).rearrange("w (n h) -> w n h", h=HALVES),
                in_=g_flipped[:].rearrange("w (h n) -> w n h", h=HALVES),
            )
            grouped_of[unit] = g_grouped

        def quantise_unit(unit):
            cols = slice(unit * P, (unit + 1) * P)
            nc.vector.quantize_mx(
                out=g_codes[:, cols].bitcast(E5M2_X4),
                scales=g_scales[:, cols],
                in_=grouped_of[unit][:],
            )

        def passes(block):
            sums = sum_banks.tile([P, N_MOVING], F32)
            for hop in range(HOPS):
                unit = block * HOPS + hop
                cols = slice(unit * P, (unit + 1) * P)
                first = (W2_BLOCK - hop) * P
                window = slice(first, first + N_MOVING)
                nc.tensor.matmul_mx(
                    out=sums[:],
                    lhsT=g_codes[:, cols].bitcast(E5M2_X4),
                    lhsT_scale=g_scales[:, cols],
                    rhs=w_codes[:, window].bitcast(E4M3_X4),
                    rhs_scale=w_scales[:, window],
                    start=(hop == 0),
                    stop=(hop == HOPS - 1),
                )
            return sums

        def leave(block, sums, pieces, engines, queues):
            result = stream.tile([P, HOPS * P], F32)
            out_rows = out[block * P : (block + 1) * P, :, :].rearrange("n p d -> n (p d)")
            width = HOPS * P // pieces
            for piece in range(pieces):
                cols = slice(piece * width, (piece + 1) * width)
                engines[piece % len(engines)](out=result[:, cols], in_=sums[:, cols])
                queues[piece % len(queues)].dma_start(out=out_rows[:, cols], in_=result[:, cols])

        flip_w1()
        idle_matmuls(1)
        flip_w2()
        quantise_w(4)
        quantise_w(3)
        quantise_w(2)
        quantise_w(1)
        quantise_w(0)
        idle_matmuls(1)
        flip_unit(0, False)
        quantise_unit(0)
        flip_unit(1, False)
        quantise_unit(1)
        idle_matmuls(1)
        flip_unit(2, False)
        quantise_unit(2)
        flip_unit(3, False)
        quantise_unit(3)
        idle_matmuls(1)
        flip_unit(4, False)
        quantise_unit(4)
        flip_unit(5, False)
        quantise_unit(5)
        leave(0, passes(0), 1, (nc.vector.tensor_copy,), (nc.sync,))
        flip_unit(6, False)
        quantise_unit(6)
        flip_unit(7, False)
        quantise_unit(7)
        flip_unit(8, False)
        quantise_unit(8)
        leave(1, passes(1), 1, (nc.vector.tensor_copy,), (nc.sync,))
        flip_unit(9, False)
        quantise_unit(9)
        flip_unit(10, False)
        quantise_unit(10)
        flip_unit(11, False)
        quantise_unit(11)
        leave(2, passes(2), 1, (nc.vector.tensor_copy,), (nc.sync,))
        leave(3, passes(3), 1, (nc.vector.tensor_copy,), (nc.sync,))
